import numpy as np
import ml_dtypes


def mxq(x, axis, fmt="e4m3"):
    dtype, down = {"e4m3": (ml_dtypes.float8_e4m3fn, 7), "e5m2": (ml_dtypes.float8_e5m2, 14)}[fmt]
    v = np.moveaxis(np.asarray(x, np.float32).astype(ml_dtypes.bfloat16).astype(np.float64), axis, -1)
    blocks = v.reshape(v.shape[:-1] + (-1, 32))
    amax = np.abs(blocks).max(-1, keepdims=True)
    byte = np.maximum(np.where(amax > 0, np.frexp(amax)[1] - 1 + 127, 0) - down, 1)
    scale = np.exp2(byte - 127.0)
    codes = (blocks / scale).astype(np.float32).astype(dtype).astype(np.float64)
    return np.moveaxis((codes * scale).reshape(v.shape), -1, axis)


WIDE = False


def mx_kscale(k):
    if not WIDE:
        return np.ones(k)
    levels = np.array([10, -10, 5, -5, 0])
    if k % 512:
        return np.exp2(np.random.permutation(np.resize(levels, k // 32))).repeat(32)
    a = np.empty((k // 512, 16))
    for p in range(k // 512):
        a[p, :8] = np.random.permutation(np.resize(levels, 8))
        for g in range(8):
            far = levels[np.abs(levels - a[p, g]) >= 10]
            a[p, g + 8] = far[np.random.randint(len(far))]
    return np.exp2(a.ravel()).repeat(32)


BF16 = ml_dtypes.bfloat16


def bf(x):
    return np.asarray(x, np.float32).astype(BF16)


def f64(x):
    return np.asarray(x).astype(np.float64)


B, N, D, F = 4, 64, 512, 128


def setup_inputs():
    s, t = mx_kscale(D), mx_kscale(D)
    ss = np.concatenate([s, s])
    sst = np.concatenate([s, s, t])
    return {
        'text_embedding': bf(np.random.standard_normal((B, N, D)) * s),
        'W_rel': bf(np.random.standard_normal((2 * D, D)) / np.sqrt(2 * D) / ss[:, None] * t),
        'b_rel': bf(np.random.standard_normal(D) * 0.3 * t),
        'W_go': bf(np.random.standard_normal((D, D)) / np.sqrt(D) / s[:, None]),
        'b_go': bf(np.random.standard_normal(D) * 0.3),
        'W_gr': bf(np.random.standard_normal((3 * D, F)) * 1.5 / np.sqrt(3 * D) / sst[:, None]),
        'b_gr': bf(np.random.standard_normal(F) * 0.3),
    }


def reference(text_embedding, W_rel, b_rel, W_go, b_go, W_gr, b_gr):
    xq = mxq(f64(text_embedding), 2, 'e4m3')
    wr, wg = f64(W_rel), f64(W_gr)
    new_x = np.tanh((xq @ mxq(f64(W_go), 0, 'e4m3')) + f64(b_go))
    rel0 = ((xq @ mxq(wr[:D], 0, 'e4m3'))[:, :, None, :]
            + (xq @ mxq(wr[D:], 0, 'e4m3'))[:, None, :, :] + f64(b_rel))
    pre = ((xq @ mxq(wg[:D], 0, 'e4m3'))[:, :, None, :]
           + (xq @ mxq(wg[D:2 * D], 0, 'e4m3'))[:, None, :, :]
           + (mxq(rel0, 3, 'e4m3') @ mxq(wg[2 * D:], 0, 'e4m3')) + f64(b_gr))
    return new_x, np.tanh(pre)

@@ -1,0 +1,312 @@
+from contextlib import ExitStack
+
+import concourse.mybir as mybir
+from concourse.masks import make_identity
+
+F32 = mybir.dt.float32
+BF16 = mybir.dt.bfloat16
+I32 = mybir.dt.int32
+U8 = mybir.dt.uint8
+FP8X4 = mybir.dt.float8_e4m3fn_x4
+ADD = mybir.AluOpType.add
+ACT = mybir.ActivationFunctionType
+
+P = 128
+FLOPS = 2 * 256 * 512 * (3 * 512 + 2 * 128) + 2 * 16384 * 512 * 128
+
+
+def schedule():
+    cycles = []
+    for c in range(10):
+        cycles.append(([(24 * c, 8), (24 * c + 8, 8)], [(24 * c + 16, 8)]))
+    cycles.append(([(240, 8)], [(248, 4)]))
+    cycles.append(([(252, 4)], []))
+    return cycles
+NODE_AT = 2
+
+
+def tile_languagemsgencoder_pa_t_kernel(
+    tc, text_embedding, W_rel, b_rel, W_go, b_go, W_gr, b_gr, out_0, out_1
+):
+    nc = tc.nc
+    out0_flat = out_0.rearrange("b n d -> (b n) d")
+    out1_flat = out_1.rearrange("b i j f -> (b i j) f")
+
+    def mx(out, l_codes, l_scales, r_codes, r_scales, start, stop):
+        nc.tensor.matmul_mx(
+            out=out,
+            lhsT=l_codes.bitcast(FP8X4),
+            lhsT_scale=l_scales,
+            rhs=r_codes.bitcast(FP8X4),
+            rhs_scale=r_scales,
+            start=start,
+            stop=stop,
+        )
+
+    def quantise(codes, scales, grouped):
+        nc.vector.quantize_mx(out=codes.bitcast(FP8X4), scales=scales, in_=grouped)
+
+    def regroup_views(dst, src):
+        return (
+            dst.rearrange("p (c i) t -> p c t i", i=4),
+            src.rearrange("p t (c i) -> p c t i", i=4),
+        )
+
+    def permuted_views(dst, src, lo, hi):
+        return (
+            dst.rearrange("p (t m) j -> p t m j", t=4)[:, :, lo:hi, :],
+            src.rearrange("p j (m t) -> p t m j", t=4)[:, :, lo:hi, :],
+        )
+
+    with ExitStack() as ctx:
+        const = ctx.enter_context(tc.tile_pool(name="const", bufs=1))
+        relp = ctx.enter_context(tc.tile_pool(name="relp", bufs=1))
+        codp = ctx.enter_context(tc.tile_pool(name="codp", bufs=8))
+        outp = ctx.enter_context(tc.tile_pool(name="outp", bufs=4))
+        thp = ctx.enter_context(tc.tile_pool(name="thp", bufs=8))
+        atp = ctx.enter_context(tc.psum_pool(name="atp", bufs=1))
+        hd = ctx.enter_context(tc.psum_pool(name="hd", bufs=2))
+        accp = ctx.enter_context(tc.psum_pool(name="accp", bufs=2))
+        trp = ctx.enter_context(tc.psum_pool(name="trp", bufs=2))
+        ctx.enter_context(tc.manual_schedule())
+
+        x_sb = const.tile([P, 2, 512], BF16)
+        wrel_raw = const.tile([P, 8, 512], BF16)
+        wgr_raw = const.tile([P, 12, 128], BF16)
+        wgo_raw = const.tile([P, 4, 512], BF16)
+        brel_sb = const.tile([P, 4], BF16)
+        bgo_sb = const.tile([P, 4], BF16)
+        bgr_sb = const.tile([P, 1], BF16)
+        x_scales = const.tile([P, 256], U8, align_bytes=64)
+
+        nc.vector.memset(x_scales[:].bitcast(I32), 0)
+
+        nc.sync.dma_start(
+            out=x_sb[:],
+            in_=text_embedding.rearrange("b n d -> (b n) d").rearrange("(a p) d -> p a d", p=P),
+        )
+        nc.sync.dma_start(out=wrel_raw[:, 0:4, :], in_=W_rel[0:512, :].rearrange("(p t) c -> p t c", t=4))
+        nc.sync.dma_start(out=wrel_raw[:, 4:8, :], in_=W_rel[512:1024, :].rearrange("(p t) c -> p t c", t=4))
+        nc.scalar.dma_start(out=brel_sb[:], in_=b_rel.rearrange("(p t) -> p t", t=4))
+        nc.scalar.dma_start(out=bgo_sb[:], in_=b_go.rearrange("(p t) -> p t", t=4))
+        nc.scalar.dma_start(out=bgr_sb[:], in_=b_gr.rearrange("(p o) -> p o", o=1))
+        for h in range(3):
+            nc.sync.dma_start(
+                out=wgr_raw[:, 4 * h:4 * h + 4, :],
+                in_=W_gr[512 * h:512 * (h + 1), :].rearrange("(p t) c -> p t c", t=4),
+            )
+        nc.sync.dma_start(out=wgo_raw[:], in_=W_go.rearrange("(p t) c -> p t c", t=4))
+
+        ident_f = const.tile([P, P], F32)
+        make_identity(nc, ident_f[:])
+
+        xt_ps = hd.tile([P, 2, 256], F32, tag="hd")
+        for a in range(2):
+            words = x_sb[:, a, :].bitcast(F32)
+            for u in range(2):
+                nc.tensor.transpose(xt_ps[:, u, a * P:(a + 1) * P], words[:, u:256:2], ident_f[:])
+        x_grp = const.tile([P, 256, 4], BF16, align_bytes=64)
+        x_codes = const.tile([P, 256], I32, align_bytes=64)
+        nc.vector.tensor_copy(
+            out=x_grp[:].rearrange("p n t -> p (n t)").bitcast(F32).rearrange("p (n u) -> p n u", u=2),
+            in_=xt_ps[:].rearrange("p u n -> p n u"),
+        )
+
+        wrel_grp = const.tile([P, 2, 512, 4], BF16, align_bytes=64)
+        wrel_codes = const.tile([P, 2, 512], I32, align_bytes=64)
+        wrel_scales = const.tile([P, 2, 512], U8, align_bytes=64)
+        SPLITS = (32, 48)
+        for h in range(2):
+            d, s = permuted_views(wrel_grp[:, h], wrel_raw[:, 4 * h:4 * h + 4, :], 0, SPLITS[h])
+            nc.scalar.copy(out=d, in_=s)
+            d, s = permuted_views(wrel_grp[:, h], wrel_raw[:, 4 * h:4 * h + 4, :], SPLITS[h], P)
+            nc.vector.tensor_copy(out=d, in_=s)
+            if h == 0:
+                quantise(x_codes[:], x_scales[:], x_grp[:].rearrange("p n t -> p (n t)"))
+            quantise(wrel_codes[:, h, :], wrel_scales[:, h, :], wrel_grp[:, h].rearrange("p c t -> p (c t)"))
+
+        wgr_grp = const.tile([P, 3, 128, 4], BF16, align_bytes=64)
+        wgr_codes = const.tile([P, 3, 128], I32, align_bytes=64)
+        wgr_scales = const.tile([P, 3, 128], U8, align_bytes=64)
+
+        bt_ps = []
+        at_sb = const.tile([P, 256, 4], F32)
+        bt_sb = const.tile([P, 256, 4], F32)
+
+        head_ps = {}
+
+        def first_relation(a):
+            xc, xs = x_codes[:, a * P:(a + 1) * P], x_scales[:, a * P:(a + 1) * P]
+            bt_a = atp.tile([P, 4, P], F32, name="bt%d" % a)
+            bt_ps.append(bt_a)
+            at_tmp = hd.tile([P, 4, P], F32, name="at_tmp", tag="hd")
+            bt_tmp = hd.tile([P, 4, P], F32, name="bt_tmp", tag="hd")
+            head_ps[a] = (at_tmp, bt_tmp)
+            for dst, h in ((at_tmp, 0), (bt_a, 1), (bt_tmp, 1)):
+                for t in range(4):
+                    mx(dst[:, t, :], wrel_codes[:, h, t * P:(t + 1) * P], wrel_scales[:, h, t * P:(t + 1) * P],
+                       xc, xs, True, True)
+
+        def first_relation_out(a):
+            at_tmp, bt_tmp = head_ps[a]
+            nc.vector.tensor_tensor(
+                out=at_sb[:, a * P:(a + 1) * P, :],
+                in0=at_tmp[:].rearrange("p t n -> p n t"),
+                in1=brel_sb[:].unsqueeze(1).to_broadcast([P, P, 4]),
+                op=ADD,
+            )
+            nc.scalar.copy(out=bt_sb[:, a * P:(a + 1) * P, :], in_=bt_tmp[:].rearrange("p t n -> p n t"))
+
+        wgo_grp = const.tile([P, 512, 4], BF16, align_bytes=64)
+        for h in range(3):
+            d, s = regroup_views(wgr_grp[:, h], wgr_raw[:, 4 * h:4 * h + 4, :])
+            nc.scalar.copy(out=d, in_=s)
+
+        first_relation(0)
+        first_relation_out(0)
+        d, s = permuted_views(wgo_grp[:], wgo_raw[:], 0, P)
+        nc.scalar.copy(out=d, in_=s)
+
+        xj_codes = const.tile([P, 4, 256], I32, align_bytes=64)
+        xj_scales = const.tile([P, 4, 256], U8, align_bytes=64)
+        nc.vector.tensor_copy(
+            out=xj_codes[:].rearrange("p b (i j) -> p b i j", i=4),
+            in_=x_codes[:].rearrange("p (b j) -> p b j", b=4).unsqueeze(2).to_broadcast([P, 4, 4, 64]),
+        )
+        first_relation(1)
+        ptb_sb = const.tile([P, 256], F32)
+
+        def second_stage_operands():
+            nc.vector.tensor_copy(
+                out=xj_scales[:].rearrange("p b c -> p (b c)").bitcast(I32).rearrange(
+                    "p (b i j) -> p b i j", b=4, i=4),
+                in_=x_scales[:].bitcast(I32).rearrange("p (b j) -> p b j", b=4).unsqueeze(2).to_broadcast(
+                    [P, 4, 4, 16]),
+            )
+            for h in range(3):
+                quantise(wgr_codes[:, h, :], wgr_scales[:, h, :], wgr_grp[:, h].rearrange("p c t -> p (c t)"))
+            pt_ps = hd.tile([P, 256], F32, tag="hd")
+            mx(pt_ps[:], wgr_codes[:, 0, :], wgr_scales[:, 0, :], x_codes[:], x_scales[:], True, True)
+            nc.scalar.activation(out=ptb_sb[:], in_=pt_ps[:], func=ACT.Identity, bias=bgr_sb[:], scale=1.0)
+
+        rel_bf = {}
+        rel_codes = {}
+        rel_scales = {}
+        th_sb = {}
+
+        def build(u, on_gpsimd, slot):
+            tok0, n = u
+            b = tok0 // 64
+            c0 = (b % 2) * 64
+            in0 = at_sb[:, tok0:tok0 + n, :].unsqueeze(2).to_broadcast([P, n, 64, 4])
+            if on_gpsimd:
+                rel_bf[u] = relp.tile([P, n * 256], BF16, name="rel_g", tag=slot, align_bytes=64)
+                nc.gpsimd.tensor_tensor(
+                    out=rel_bf[u][:].rearrange("p (i j t) -> p i j t", i=n, j=64),
+                    in0=in0,
+                    in1=bt_sb[:, b * 64:(b + 1) * 64, :].unsqueeze(1).to_broadcast([P, n, 64, 4]),
+                    op=ADD,
+                )
+            else:
+                rel_bf[u] = relp.tile([P, n * 256], BF16, name="rel_v", tag=slot, align_bytes=64)
+                nc.vector.tensor_tensor(
+                    out=rel_bf[u][:].rearrange("p (i j t) -> p i j t", i=n, j=64),
+                    in0=in0,
+                    in1=bt_ps[b // 2][:, :, c0:c0 + 64].rearrange("p t j -> p j t").unsqueeze(1).to_broadcast(
+                        [P, n, 64, 4]),
+                    op=ADD,
+                )
+
+        def quant(u):
+            n = u[1]
+            rel_codes[u] = codp.tile([P, n * 64], I32, name="rel_codes", tag="rel_codes", align_bytes=64)
+            rel_scales[u] = codp.tile([P, n * 64], U8, name="rel_scales", tag="rel_scales", align_bytes=64)
+            quantise(rel_codes[u][:], rel_scales[u][:], rel_bf[u][:])
+
+        def product(u):
+            tok0, n = u
+            b = tok0 // 64
+            acc = accp.tile([P, n * 64], F32, name="acc", tag="acc")
+            for hf in range(n // 4):
+                cols = slice(hf * 256, (hf + 1) * 256)
+                mx(acc[:, cols], wgr_codes[:, 1, :], wgr_scales[:, 1, :], xj_codes[:, b, :], xj_scales[:, b, :],
+                   True, False)
+                mx(acc[:, cols], wgr_codes[:, 2, :], wgr_scales[:, 2, :], rel_codes[u][:, cols],
+                   rel_scales[u][:, cols], False, True)
+            th_sb[u] = thp.tile([P, n * 64], F32, name="th", tag="th")
+            for i in range(n):
+                tok = tok0 + i
+                nc.scalar.activation(out=th_sb[u][:, i * 64:(i + 1) * 64], in_=acc[:, i * 64:(i + 1) * 64],
+                                     func=ACT.Tanh, bias=ptb_sb[:, tok:tok + 1], scale=1.0)
+
+        tr_ps = {}
+
+        def turn(u):
+            n = u[1]
+            tr_ps[u] = trp.tile([P, n * 64], F32, name="tr", tag="tr")
+            for k in range(n // 2):
+                nc.tensor.transpose(tr_ps[u][:, k * P:(k + 1) * P], th_sb[u][:, k * P:(k + 1) * P], ident_f[:])
+
+        def store(u, on_vector):
+            tok0, n = u
+            tr = tr_ps[u]
+            o_sb = outp.tile([P, n // 2, P], F32, name="o_sb", tag="o_sb")
+            if on_vector:
+                nc.vector.tensor_copy(out=o_sb[:].rearrange("p k f -> p (k f)"), in_=tr[:])
+            else:
+                nc.scalar.copy(out=o_sb[:].rearrange("p k f -> p (k f)"), in_=tr[:])
+            nc.sync.dma_start(
+                out=out1_flat[tok0 * 64:(tok0 + n) * 64, :].rearrange("(k m) f -> m k f", m=P), in_=o_sb[:]
+            )
+
+        wgo_codes = const.tile([P, 512], I32, align_bytes=64)
+        wgo_scales = const.tile([P, 512], U8, align_bytes=64)
+        nxt_sb = const.tile([P, 4, 256], F32)
+
+        def node_update():
+            for t in range(4):
+                nx_ps = hd.tile([P, 256], F32, name="nx_ps", tag="hd")
+                mx(nx_ps[:], wgo_codes[:, t * P:(t + 1) * P], wgo_scales[:, t * P:(t + 1) * P],
+                   x_codes[:], x_scales[:], True, True)
+                nc.scalar.activation(out=nxt_sb[:, t, :], in_=nx_ps[:], func=ACT.Tanh,
+                                     bias=bgo_sb[:, t:t + 1], scale=1.0)
+            for a in range(2):
+                nxr_ps = hd.tile([P, 512], F32, name="nxr_ps", tag="hd")
+                for t in range(4):
+                    nc.tensor.transpose(nxr_ps[:, t * P:(t + 1) * P], nxt_sb[:, t, a * P:(a + 1) * P], ident_f[:])
+                nx_sb = outp.tile([P, 512], F32, name="nx_sb", tag="nx_sb")
+                nc.scalar.copy(
+                    out=nx_sb[:].rearrange("p (m t) -> p m t", t=4), in_=nxr_ps[:].rearrange("p (t m) -> p m t", t=4)
+                )
+                nc.sync.dma_start(out=out0_flat[a * P:(a + 1) * P, :], in_=nx_sb[:])
+
+        previous = []
+        cycles = schedule()
+        last = len(cycles) - 1
+        for c, (v_units, g_units) in enumerate(cycles):
+            units = v_units + g_units
+            slot_g, slot_v2 = ("relZ", "relY") if c % 2 == 0 else ("relY", "relZ")
+            for u in g_units:
+                build(u, True, slot_g)
+            for u, slot in zip(v_units, ("relX", slot_v2)):
+                build(u, False, slot)
+            if c == 0:
+                first_relation_out(1)
+                second_stage_operands()
+                quantise(wgo_codes[:], wgo_scales[:], wgo_grp[:].rearrange("p c t -> p (c t)"))
+            for u in previous:
+                turn(u)
+                if c < last:
+                    store(u, False)
+            for u in units:
+                quant(u)
+            for u in units:
+                product(u)
+            if c == last:
+                for u in previous:
+                    store(u, True)
+                turn(units[0])
+                store(units[0], True)
+            if c == NODE_AT:
+                node_update()
+            previous = units

@@ -16,13 +16,12 @@ FLOPS = 2 * 256 * 512 * (3 * 512 + 2 * 128) + 2 * 16384 * 512 * 128
 
 
 def schedule():
-    cycles = []
-    for c in range(10):
+    cycles = [([(0, 4)], []), ([(4, 4), (16, 8)], [(8, 8)])]
+    for c in range(1, 10):
         cycles.append(([(24 * c, 8), (24 * c + 8, 8)], [(24 * c + 16, 8)]))
     cycles.append(([(240, 8)], [(248, 4)]))
     cycles.append(([(252, 4)], []))
     return cycles
-NODE_AT = 2
 
 
 def tile_languagemsgencoder_pa_t_kernel(
@@ -65,9 +64,7 @@ def tile_languagemsgencoder_pa_t_kernel(
         outp = ctx.enter_context(tc.tile_pool(name="outp", bufs=4))
         thp = ctx.enter_context(tc.tile_pool(name="thp", bufs=8))
         atp = ctx.enter_context(tc.psum_pool(name="atp", bufs=1))
-        hd = ctx.enter_context(tc.psum_pool(name="hd", bufs=2))
-        accp = ctx.enter_context(tc.psum_pool(name="accp", bufs=2))
-        trp = ctx.enter_context(tc.psum_pool(name="trp", bufs=2))
+        psp = ctx.enter_context(tc.psum_pool(name="psp", bufs=6))
         ctx.enter_context(tc.manual_schedule())
 
         x_sb = const.tile([P, 2, 512], BF16)
@@ -87,20 +84,20 @@ def tile_languagemsgencoder_pa_t_kernel(
         )
         nc.sync.dma_start(out=wrel_raw[:, 0:4, :], in_=W_rel[0:512, :].rearrange("(p t) c -> p t c", t=4))
         nc.sync.dma_start(out=wrel_raw[:, 4:8, :], in_=W_rel[512:1024, :].rearrange("(p t) c -> p t c", t=4))
-        nc.scalar.dma_start(out=brel_sb[:], in_=b_rel.rearrange("(p t) -> p t", t=4))
-        nc.scalar.dma_start(out=bgo_sb[:], in_=b_go.rearrange("(p t) -> p t", t=4))
-        nc.scalar.dma_start(out=bgr_sb[:], in_=b_gr.rearrange("(p o) -> p o", o=1))
+        nc.sync.dma_start(out=brel_sb[:], in_=b_rel.rearrange("(p t) -> p t", t=4))
         for h in range(3):
             nc.sync.dma_start(
                 out=wgr_raw[:, 4 * h:4 * h + 4, :],
                 in_=W_gr[512 * h:512 * (h + 1), :].rearrange("(p t) c -> p t c", t=4),
             )
         nc.sync.dma_start(out=wgo_raw[:], in_=W_go.rearrange("(p t) c -> p t c", t=4))
+        nc.sync.dma_start(out=bgr_sb[:], in_=b_gr.rearrange("(p o) -> p o", o=1))
+        nc.sync.dma_start(out=bgo_sb[:], in_=b_go.rearrange("(p t) -> p t", t=4))
 
         ident_f = const.tile([P, P], F32)
         make_identity(nc, ident_f[:])
 
-        xt_ps = hd.tile([P, 2, 256], F32, tag="hd")
+        xt_ps = psp.tile([P, 2, 256], F32, tag="ps")
         for a in range(2):
             words = x_sb[:, a, :].bitcast(F32)
             for u in range(2):
@@ -139,8 +136,8 @@ def tile_languagemsgencoder_pa_t_kernel(
             xc, xs = x_codes[:, a * P:(a + 1) * P], x_scales[:, a * P:(a + 1) * P]
             bt_a = atp.tile([P, 4, P], F32, name="bt%d" % a)
             bt_ps.append(bt_a)
-            at_tmp = hd.tile([P, 4, P], F32, name="at_tmp", tag="hd")
-            bt_tmp = hd.tile([P, 4, P], F32, name="bt_tmp", tag="hd")
+            at_tmp = psp.tile([P, 4, P], F32, name="at_tmp", tag="ps")
+            bt_tmp = psp.tile([P, 4, P], F32, name="bt_tmp", tag="ps")
             head_ps[a] = (at_tmp, bt_tmp)
             for dst, h in ((at_tmp, 0), (bt_a, 1), (bt_tmp, 1)):
                 for t in range(4):
@@ -185,7 +182,7 @@ def tile_languagemsgencoder_pa_t_kernel(
             )
             for h in range(3):
                 quantise(wgr_codes[:, h, :], wgr_scales[:, h, :], wgr_grp[:, h].rearrange("p c t -> p (c t)"))
-            pt_ps = hd.tile([P, 256], F32, tag="hd")
+            pt_ps = psp.tile([P, 256], F32, tag="ps")
             mx(pt_ps[:], wgr_codes[:, 0, :], wgr_scales[:, 0, :], x_codes[:], x_scales[:], True, True)
             nc.scalar.activation(out=ptb_sb[:], in_=pt_ps[:], func=ACT.Identity, bias=bgr_sb[:], scale=1.0)
 
@@ -226,7 +223,7 @@ def tile_languagemsgencoder_pa_t_kernel(
         def product(u):
             tok0, n = u
             b = tok0 // 64
-            acc = accp.tile([P, n * 64], F32, name="acc", tag="acc")
+            acc = psp.tile([P, n * 64], F32, name="acc", tag="ps")
             for hf in range(n // 4):
                 cols = slice(hf * 256, (hf + 1) * 256)
                 mx(acc[:, cols], wgr_codes[:, 1, :], wgr_scales[:, 1, :], xj_codes[:, b, :], xj_scales[:, b, :],
@@ -243,7 +240,7 @@ def tile_languagemsgencoder_pa_t_kernel(
 
         def turn(u):
             n = u[1]
-            tr_ps[u] = trp.tile([P, n * 64], F32, name="tr", tag="tr")
+            tr_ps[u] = psp.tile([P, n * 64], F32, name="tr", tag="ps")
             for k in range(n // 2):
                 nc.tensor.transpose(tr_ps[u][:, k * P:(k + 1) * P], th_sb[u][:, k * P:(k + 1) * P], ident_f[:])
 
@@ -263,15 +260,17 @@ def tile_languagemsgencoder_pa_t_kernel(
         wgo_scales = const.tile([P, 512], U8, align_bytes=64)
         nxt_sb = const.tile([P, 4, 256], F32)
 
-        def node_update():
+        def node_update_tanh():
             for t in range(4):
-                nx_ps = hd.tile([P, 256], F32, name="nx_ps", tag="hd")
+                nx_ps = psp.tile([P, 256], F32, name="nx_ps", tag="ps")
                 mx(nx_ps[:], wgo_codes[:, t * P:(t + 1) * P], wgo_scales[:, t * P:(t + 1) * P],
                    x_codes[:], x_scales[:], True, True)
                 nc.scalar.activation(out=nxt_sb[:, t, :], in_=nx_ps[:], func=ACT.Tanh,
                                      bias=bgo_sb[:, t:t + 1], scale=1.0)
+
+        def node_update_out():
             for a in range(2):
-                nxr_ps = hd.tile([P, 512], F32, name="nxr_ps", tag="hd")
+                nxr_ps = psp.tile([P, 512], F32, name="nxr_ps", tag="ps")
                 for t in range(4):
                     nc.tensor.transpose(nxr_ps[:, t * P:(t + 1) * P], nxt_sb[:, t, a * P:(a + 1) * P], ident_f[:])
                 nx_sb = outp.tile([P, 512], F32, name="nx_sb", tag="nx_sb")
@@ -288,12 +287,14 @@ def tile_languagemsgencoder_pa_t_kernel(
             slot_g, slot_v2 = ("relZ", "relY") if c % 2 == 0 else ("relY", "relZ")
             for u in g_units:
                 build(u, True, slot_g)
-            for u, slot in zip(v_units, ("relX", slot_v2)):
+            for u, slot in zip(v_units, ("relX", slot_v2) if len(v_units) == 2 or c == 0 else (slot_v2,)):
                 build(u, False, slot)
             if c == 0:
-                first_relation_out(1)
                 second_stage_operands()
+            if c == 1:
+                first_relation_out(1)
                 quantise(wgo_codes[:], wgo_scales[:], wgo_grp[:].rearrange("p c t -> p (c t)"))
+                node_update_tanh()
             for u in previous:
                 turn(u)
                 if c < last:
@@ -307,6 +308,6 @@ def tile_languagemsgencoder_pa_t_kernel(
                     store(u, True)
                 turn(units[0])
                 store(units[0], True)
-            if c == NODE_AT:
-                node_update()
+            if c == 2:
+                node_update_out()
             previous = units

@@ -61,7 +61,7 @@ def tile_languagemsgencoder_pa_t_kernel(
         const = ctx.enter_context(tc.tile_pool(name="const", bufs=1))
         relp = ctx.enter_context(tc.tile_pool(name="relp", bufs=1))
         codp = ctx.enter_context(tc.tile_pool(name="codp", bufs=8))
-        outp = ctx.enter_context(tc.tile_pool(name="outp", bufs=4))
+        outp = ctx.enter_context(tc.tile_pool(name="outp", bufs=12))
         thp = ctx.enter_context(tc.tile_pool(name="thp", bufs=8))
         atp = ctx.enter_context(tc.psum_pool(name="atp", bufs=1))
         psp = ctx.enter_context(tc.psum_pool(name="psp", bufs=6))
@@ -78,11 +78,11 @@ def tile_languagemsgencoder_pa_t_kernel(
 
         nc.vector.memset(x_scales[:].bitcast(I32), 0)
 
+        nc.sync.dma_start(out=wrel_raw[:, 0:4, :], in_=W_rel[0:512, :].rearrange("(p t) c -> p t c", t=4))
         nc.sync.dma_start(
             out=x_sb[:],
             in_=text_embedding.rearrange("b n d -> (b n) d").rearrange("(a p) d -> p a d", p=P),
         )
-        nc.sync.dma_start(out=wrel_raw[:, 0:4, :], in_=W_rel[0:512, :].rearrange("(p t) c -> p t c", t=4))
         nc.sync.dma_start(out=wrel_raw[:, 4:8, :], in_=W_rel[512:1024, :].rearrange("(p t) c -> p t c", t=4))
         nc.sync.dma_start(out=brel_sb[:], in_=b_rel.rearrange("(p t) -> p t", t=4))
         for h in range(3):
@@ -104,23 +104,30 @@ def tile_languagemsgencoder_pa_t_kernel(
                 nc.tensor.transpose(xt_ps[:, u, a * P:(a + 1) * P], words[:, u:256:2], ident_f[:])
         x_grp = const.tile([P, 256, 4], BF16, align_bytes=64)
         x_codes = const.tile([P, 256], I32, align_bytes=64)
-        nc.vector.tensor_copy(
-            out=x_grp[:].rearrange("p n t -> p (n t)").bitcast(F32).rearrange("p (n u) -> p n u", u=2),
-            in_=xt_ps[:].rearrange("p u n -> p n u"),
-        )
 
         wrel_grp = const.tile([P, 2, 512, 4], BF16, align_bytes=64)
         wrel_codes = const.tile([P, 2, 512], I32, align_bytes=64)
         wrel_scales = const.tile([P, 2, 512], U8, align_bytes=64)
-        SPLITS = (32, 48)
-        for h in range(2):
+        SPLITS = (48, 40)
+
+        def regroup_wrel(h):
             d, s = permuted_views(wrel_grp[:, h], wrel_raw[:, 4 * h:4 * h + 4, :], 0, SPLITS[h])
             nc.scalar.copy(out=d, in_=s)
             d, s = permuted_views(wrel_grp[:, h], wrel_raw[:, 4 * h:4 * h + 4, :], SPLITS[h], P)
             nc.vector.tensor_copy(out=d, in_=s)
-            if h == 0:
-                quantise(x_codes[:], x_scales[:], x_grp[:].rearrange("p n t -> p (n t)"))
+
+        def quantise_wrel(h):
             quantise(wrel_codes[:, h, :], wrel_scales[:, h, :], wrel_grp[:, h].rearrange("p c t -> p (c t)"))
+
+        regroup_wrel(0)
+        nc.scalar.copy(
+            out=x_grp[:].rearrange("p n t -> p (n t)").bitcast(F32).rearrange("p (n u) -> p n u", u=2),
+            in_=xt_ps[:].rearrange("p u n -> p n u"),
+        )
+        quantise_wrel(0)
+        regroup_wrel(1)
+        quantise(x_codes[:], x_scales[:], x_grp[:].rearrange("p n t -> p (n t)"))
+        quantise_wrel(1)
 
         wgr_grp = const.tile([P, 3, 128, 4], BF16, align_bytes=64)
         wgr_codes = const.tile([P, 3, 128], I32, align_bytes=64)
@@ -139,7 +146,7 @@ def tile_languagemsgencoder_pa_t_kernel(
             at_tmp = psp.tile([P, 4, P], F32, name="at_tmp", tag="ps")
             bt_tmp = psp.tile([P, 4, P], F32, name="bt_tmp", tag="ps")
             head_ps[a] = (at_tmp, bt_tmp)
-            for dst, h in ((at_tmp, 0), (bt_a, 1), (bt_tmp, 1)):
+            for dst, h in ((at_tmp, 0), (bt_tmp, 1), (bt_a, 1)):
                 for t in range(4):
                     mx(dst[:, t, :], wrel_codes[:, h, t * P:(t + 1) * P], wrel_scales[:, h, t * P:(t + 1) * P],
                        xc, xs, True, True)
@@ -160,31 +167,31 @@ def tile_languagemsgencoder_pa_t_kernel(
             nc.scalar.copy(out=d, in_=s)
 
         first_relation(0)
-        first_relation_out(0)
-        d, s = permuted_views(wgo_grp[:], wgo_raw[:], 0, P)
-        nc.scalar.copy(out=d, in_=s)
-
         xj_codes = const.tile([P, 4, 256], I32, align_bytes=64)
         xj_scales = const.tile([P, 4, 256], U8, align_bytes=64)
         nc.vector.tensor_copy(
             out=xj_codes[:].rearrange("p b (i j) -> p b i j", i=4),
             in_=x_codes[:].rearrange("p (b j) -> p b j", b=4).unsqueeze(2).to_broadcast([P, 4, 4, 64]),
         )
+        first_relation_out(0)
+        d, s = permuted_views(wgo_grp[:], wgo_raw[:], 0, P)
+        nc.scalar.copy(out=d, in_=s)
+
         first_relation(1)
         ptb_sb = const.tile([P, 256], F32)
 
         def second_stage_operands():
+            for h in range(3):
+                quantise(wgr_codes[:, h, :], wgr_scales[:, h, :], wgr_grp[:, h].rearrange("p c t -> p (c t)"))
+            pt_ps = psp.tile([P, 256], F32, tag="ps")
+            mx(pt_ps[:], wgr_codes[:, 0, :], wgr_scales[:, 0, :], x_codes[:], x_scales[:], True, True)
+            nc.scalar.activation(out=ptb_sb[:], in_=pt_ps[:], func=ACT.Identity, bias=bgr_sb[:], scale=1.0)
             nc.vector.tensor_copy(
                 out=xj_scales[:].rearrange("p b c -> p (b c)").bitcast(I32).rearrange(
                     "p (b i j) -> p b i j", b=4, i=4),
                 in_=x_scales[:].bitcast(I32).rearrange("p (b j) -> p b j", b=4).unsqueeze(2).to_broadcast(
                     [P, 4, 4, 16]),
             )
-            for h in range(3):
-                quantise(wgr_codes[:, h, :], wgr_scales[:, h, :], wgr_grp[:, h].rearrange("p c t -> p (c t)"))
-            pt_ps = psp.tile([P, 256], F32, tag="ps")
-            mx(pt_ps[:], wgr_codes[:, 0, :], wgr_scales[:, 0, :], x_codes[:], x_scales[:], True, True)
-            nc.scalar.activation(out=ptb_sb[:], in_=pt_ps[:], func=ACT.Identity, bias=bgr_sb[:], scale=1.0)
 
         rel_bf = {}
         rel_codes = {}
@@ -287,20 +294,21 @@ def tile_languagemsgencoder_pa_t_kernel(
             slot_g, slot_v2 = ("relZ", "relY") if c % 2 == 0 else ("relY", "relZ")
             for u in g_units:
                 build(u, True, slot_g)
-            for u, slot in zip(v_units, ("relX", slot_v2) if len(v_units) == 2 or c == 0 else (slot_v2,)):
+            for u, slot in zip(v_units, ("relX", slot_v2) if len(v_units) == 2 else (slot_v2,)):
                 build(u, False, slot)
             if c == 0:
                 second_stage_operands()
             if c == 1:
                 first_relation_out(1)
-                quantise(wgo_codes[:], wgo_scales[:], wgo_grp[:].rearrange("p c t -> p (c t)"))
-                node_update_tanh()
             for u in previous:
                 turn(u)
                 if c < last:
                     store(u, False)
             for u in units:
                 quant(u)
+                if c == 1 and u == units[0]:
+                    quantise(wgo_codes[:], wgo_scales[:], wgo_grp[:].rearrange("p c t -> p (c t)"))
+                    node_update_tanh()
             for u in units:
                 product(u)
             if c == last:

@@ -15,12 +15,19 @@ P = 128
 FLOPS = 2 * 256 * 512 * (3 * 512 + 2 * 128) + 2 * 16384 * 512 * 128
 
 
+P_TOKENS = (232, 240, 248)
+
+
+def pieces_of(cycle):
+    return range(min(-(-4 * (cycle - 1) // 3), 12), min(-(-4 * cycle // 3), 12)) if cycle >= 1 else range(0)
+
+
 def schedule():
     cycles = [([(0, 4)], []), ([(4, 4), (16, 8)], [(8, 8)])]
-    for c in range(1, 10):
+    for c in range(1, 9):
         cycles.append(([(24 * c, 8), (24 * c + 8, 8)], [(24 * c + 16, 8)]))
-    cycles.append(([(240, 8)], [(248, 4)]))
-    cycles.append(([(252, 4)], []))
+    cycles.append(([(216, 8)], [(224, 4)]))
+    cycles.append(([(228, 4)], []))
     return cycles
 
 
@@ -72,6 +79,7 @@ def tile_languagemsgencoder_pa_t_kernel(
         wgr_raw = const.tile([P, 12, 128], BF16)
         wgo_raw = const.tile([P, 4, 512], BF16)
         brel_sb = const.tile([P, 4], BF16)
+        brel_row = const.tile([1, 512], BF16)
         bgo_sb = const.tile([P, 4], BF16)
         bgr_sb = const.tile([P, 1], BF16)
         x_scales = const.tile([P, 256], U8, align_bytes=64)
@@ -92,10 +100,22 @@ def tile_languagemsgencoder_pa_t_kernel(
             )
         nc.sync.dma_start(out=wgo_raw[:], in_=W_go.rearrange("(p t) c -> p t c", t=4))
         nc.sync.dma_start(out=bgr_sb[:], in_=b_gr.rearrange("(p o) -> p o", o=1))
+        nc.sync.dma_start(out=brel_row[:], in_=b_rel.rearrange("(o c) -> o c", o=1))
         nc.sync.dma_start(out=bgo_sb[:], in_=b_go.rearrange("(p t) -> p t", t=4))
 
         ident_f = const.tile([P, P], F32)
         make_identity(nc, ident_f[:])
+        sel = const.tile([P, 3, 512], F32)
+        i0 = P_TOKENS[0] % 64
+        nc.vector.tensor_copy(
+            out=sel[0:64].rearrange("p u (i j) -> p (u i) j", i=8),
+            in_=ident_f[0:64, i0:i0 + 24].unsqueeze(2).to_broadcast([64, 24, 64]),
+        )
+        nc.vector.tensor_copy(
+            out=sel[64:P].rearrange("p u (i j) -> p (u i) j", i=8),
+            in_=ident_f[64:P, 64:P].unsqueeze(1).to_broadcast([64, 24, 64]),
+        )
+        nc.vector.memset(sel[0:1, :, :], 1.0)
 
         xt_ps = psp.tile([P, 2, 256], F32, tag="ps")
         for a in range(2):
@@ -108,7 +128,7 @@ def tile_languagemsgencoder_pa_t_kernel(
         wrel_grp = const.tile([P, 2, 512, 4], BF16, align_bytes=64)
         wrel_codes = const.tile([P, 2, 512], I32, align_bytes=64)
         wrel_scales = const.tile([P, 2, 512], U8, align_bytes=64)
-        SPLITS = (48, 40)
+        SPLITS = (32, 24)
 
         def regroup_wrel(h):
             d, s = permuted_views(wrel_grp[:, h], wrel_raw[:, 4 * h:4 * h + 4, :], 0, SPLITS[h])
@@ -221,6 +241,36 @@ def tile_languagemsgencoder_pa_t_kernel(
                     op=ADD,
                 )
 
+        nat_sb = const.tile([P, 512], F32)
+
+        def natural_rows():
+            na_ps = psp.tile([P, 512], F32, name="na_ps", tag="ps")
+            nb_ps = psp.tile([P, 512], F32, name="nb_ps", tag="ps")
+            for dst, h in ((na_ps, 0), (nb_ps, 1)):
+                mx(dst[:], xj_codes[:, 3, 0:P], xj_scales[:, 3, 0:P], wrel_codes[:, h, :], wrel_scales[:, h, :], True, True)
+            nc.scalar.copy(out=nat_sb[0:64, :], in_=na_ps[0:64, :])
+            nc.scalar.copy(out=nat_sb[64:P, :], in_=nb_ps[64:P, :])
+            nc.scalar.copy(out=nat_sb[0:1, :].rearrange("p (t m) -> p t m", t=4),
+                           in_=brel_row[:].rearrange("p (m t) -> p t m", t=4))
+
+        piece_ps = {}
+
+        def piece_products(piece):
+            k, q = piece // 4, piece % 4
+            rp = psp.tile([P, 4, P], F32, name="rp", tag="ps")
+            piece_ps[piece] = rp
+            for t in range(4):
+                nc.tensor.matmul(rp[:, t, :], nat_sb[:, t * P:(t + 1) * P], sel[:, k, q * P:(q + 1) * P],
+                                 start=True, stop=True)
+
+        def piece_out(piece):
+            k, q = piece // 4, piece % 4
+            u = (P_TOKENS[k], 8)
+            if q == 0:
+                rel_bf[u] = relp.tile([P, 2048], BF16, name="rel_p", tag="relP%d" % (k % 2), align_bytes=64)
+            nc.scalar.copy(out=rel_bf[u][:, q * 512:(q + 1) * 512].rearrange("p (n t) -> p n t", t=4),
+                           in_=piece_ps[piece][:].rearrange("p t n -> p n t"))
+
         def quant(u):
             n = u[1]
             rel_codes[u] = codp.tile([P, n * 64], I32, name="rel_codes", tag="rel_codes", align_bytes=64)
@@ -290,7 +340,8 @@ def tile_languagemsgencoder_pa_t_kernel(
         cycles = schedule()
         last = len(cycles) - 1
         for c, (v_units, g_units) in enumerate(cycles):
-            units = v_units + g_units
+            p_units = [(P_TOKENS[c // 3 - 1], 8)] if c in (4, 7, 10) else []
+            units = p_units + v_units + g_units
             slot_g, slot_v2 = ("relZ", "relY") if c % 2 == 0 else ("relY", "relZ")
             for u in g_units:
                 build(u, True, slot_g)
@@ -298,8 +349,12 @@ def tile_languagemsgencoder_pa_t_kernel(
                 build(u, False, slot)
             if c == 0:
                 second_stage_operands()
+                natural_rows()
             if c == 1:
                 first_relation_out(1)
+            for piece in pieces_of(c):
+                piece_products(piece)
+                piece_out(piece)
             for u in previous:
                 turn(u)
                 if c < last:

@@ -15,11 +15,22 @@ P = 128
 FLOPS = 2 * 256 * 512 * (3 * 512 + 2 * 128) + 2 * 16384 * 512 * 128
 
 
-P_TOKENS = (232, 240, 248)
+P_UNITS = ((228, 8), (236, 8), (244, 8), (252, 4))
+PIECES = 14
 
 
-def pieces_of(cycle):
-    return range(min(-(-4 * (cycle - 1) // 3), 12), min(-(-4 * cycle // 3), 12)) if cycle >= 1 else range(0)
+def pieces_built(cycle):
+    return min(3 * (cycle + 1) // 2, PIECES) if cycle > 0 else 0
+
+
+def tensor_units(cycle):
+    units = []
+    end = 0
+    for u in P_UNITS:
+        end += u[1] // 2
+        if pieces_built(cycle - 2) < end <= pieces_built(cycle - 1):
+            units.append(u)
+    return units
 
 
 def schedule():
@@ -27,7 +38,6 @@ def schedule():
     for c in range(1, 9):
         cycles.append(([(24 * c, 8), (24 * c + 8, 8)], [(24 * c + 16, 8)]))
     cycles.append(([(216, 8)], [(224, 4)]))
-    cycles.append(([(228, 4)], []))
     return cycles
 
 
@@ -105,17 +115,11 @@ def tile_languagemsgencoder_pa_t_kernel(
 
         ident_f = const.tile([P, P], F32)
         make_identity(nc, ident_f[:])
-        sel = const.tile([P, 3, 512], F32)
-        i0 = P_TOKENS[0] % 64
-        nc.vector.tensor_copy(
-            out=sel[0:64].rearrange("p u (i j) -> p (u i) j", i=8),
-            in_=ident_f[0:64, i0:i0 + 24].unsqueeze(2).to_broadcast([64, 24, 64]),
-        )
-        nc.vector.tensor_copy(
-            out=sel[64:P].rearrange("p u (i j) -> p (u i) j", i=8),
-            in_=ident_f[64:P, 64:P].unsqueeze(1).to_broadcast([64, 24, 64]),
-        )
-        nc.vector.memset(sel[0:1, :, :], 1.0)
+        sel = const.tile([P, 28, 64], F32)
+        i0 = P_UNITS[0][0] % 64
+        nc.vector.tensor_copy(out=sel[0:64], in_=ident_f[0:64, i0:i0 + 28].unsqueeze(2).to_broadcast([64, 28, 64]))
+        nc.vector.tensor_copy(out=sel[64:P], in_=ident_f[64:P, 64:P].unsqueeze(1).to_broadcast([64, 28, 64]))
+        nc.vector.memset(sel[0:1], 1.0)
 
         xt_ps = psp.tile([P, 2, 256], F32, tag="ps")
         for a in range(2):
@@ -128,7 +132,7 @@ def tile_languagemsgencoder_pa_t_kernel(
         wrel_grp = const.tile([P, 2, 512, 4], BF16, align_bytes=64)
         wrel_codes = const.tile([P, 2, 512], I32, align_bytes=64)
         wrel_scales = const.tile([P, 2, 512], U8, align_bytes=64)
-        SPLITS = (32, 24)
+        SPLITS = (48, 40)
 
         def regroup_wrel(h):
             d, s = permuted_views(wrel_grp[:, h], wrel_raw[:, 4 * h:4 * h + 4, :], 0, SPLITS[h])
@@ -164,22 +168,38 @@ def tile_languagemsgencoder_pa_t_kernel(
             bt_a = atp.tile([P, 4, P], F32, name="bt%d" % a)
             bt_ps.append(bt_a)
             at_tmp = psp.tile([P, 4, P], F32, name="at_tmp", tag="ps")
-            bt_tmp = psp.tile([P, 4, P], F32, name="bt_tmp", tag="ps")
-            head_ps[a] = (at_tmp, bt_tmp)
-            for dst, h in ((at_tmp, 0), (bt_tmp, 1), (bt_a, 1)):
+            targets = [(at_tmp, 0), (bt_a, 1)]
+            if a == 0:
+                bt_tmp = psp.tile([P, 4, P], F32, name="bt_tmp", tag="ps")
+                targets.append((bt_tmp, 1))
+            head_ps[a] = (at_tmp, bt_tmp if a == 0 else bt_a)
+            for dst, h in targets:
                 for t in range(4):
                     mx(dst[:, t, :], wrel_codes[:, h, t * P:(t + 1) * P], wrel_scales[:, h, t * P:(t + 1) * P],
                        xc, xs, True, True)
 
-        def first_relation_out(a):
-            at_tmp, bt_tmp = head_ps[a]
+        def a_out(a, lo, hi):
             nc.vector.tensor_tensor(
-                out=at_sb[:, a * P:(a + 1) * P, :],
-                in0=at_tmp[:].rearrange("p t n -> p n t"),
-                in1=brel_sb[:].unsqueeze(1).to_broadcast([P, P, 4]),
+                out=at_sb[:, a * P + lo:a * P + hi, :],
+                in0=head_ps[a][0][:, :, lo:hi].rearrange("p t n -> p n t"),
+                in1=brel_sb[:].unsqueeze(1).to_broadcast([P, hi - lo, 4]),
                 op=ADD,
             )
-            nc.scalar.copy(out=bt_sb[:, a * P:(a + 1) * P, :], in_=bt_tmp[:].rearrange("p t n -> p n t"))
+
+        def b_out(a):
+            nc.scalar.copy(out=bt_sb[:, a * P:(a + 1) * P, :], in_=head_ps[a][1][:].rearrange("p t n -> p n t"))
+
+        nat_sb = const.tile([P, 512], F32)
+
+        def natural_rows():
+            na_ps = psp.tile([P, 512], F32, name="na_ps", tag="ps")
+            nb_ps = psp.tile([P, 512], F32, name="nb_ps", tag="ps")
+            for dst, h in ((na_ps, 0), (nb_ps, 1)):
+                mx(dst[:], xd_codes[:], xd_scales[:], wrel_codes[:, h, :], wrel_scales[:, h, :], True, True)
+            nc.scalar.copy(out=nat_sb[0:64, :], in_=na_ps[0:64, :])
+            nc.scalar.copy(out=nat_sb[64:P, :], in_=nb_ps[64:P, :])
+            nc.scalar.copy(out=nat_sb[0:1, :].rearrange("p (t m) -> p t m", t=4),
+                           in_=brel_row[:].rearrange("p (m t) -> p t m", t=4))
 
         wgo_grp = const.tile([P, 512, 4], BF16, align_bytes=64)
         for h in range(3):
@@ -187,16 +207,38 @@ def tile_languagemsgencoder_pa_t_kernel(
             nc.scalar.copy(out=d, in_=s)
 
         first_relation(0)
-        xj_codes = const.tile([P, 4, 256], I32, align_bytes=64)
-        xj_scales = const.tile([P, 4, 256], U8, align_bytes=64)
+        xj_codes = const.tile([P, 4, 512], I32, align_bytes=64)
+        xj_scales = const.tile([P, 4, 512], U8, align_bytes=64)
+        for b in range(1, 4):
+            nc.sync.dma_start(
+                out=xj_codes[:, b, :].rearrange("p (i j) -> p i j", i=8),
+                in_=x_codes[:, 64 * b:64 * (b + 1)].unsqueeze(1).to_broadcast([P, 8, 64]),
+            )
+            nc.sync.dma_start(
+                out=xj_scales[:, b, :].bitcast(I32).rearrange("p (i j) -> p i j", i=8),
+                in_=x_scales[:, 64 * b:64 * (b + 1)].bitcast(I32).unsqueeze(1).to_broadcast([P, 8, 16]),
+            )
         nc.vector.tensor_copy(
-            out=xj_codes[:].rearrange("p b (i j) -> p b i j", i=4),
-            in_=x_codes[:].rearrange("p (b j) -> p b j", b=4).unsqueeze(2).to_broadcast([P, 4, 4, 64]),
+            out=xj_codes[:, 0, :].rearrange("p (i j) -> p i j", i=8),
+            in_=x_codes[:, 0:64].unsqueeze(1).to_broadcast([P, 8, 64]),
         )
-        first_relation_out(0)
-        d, s = permuted_views(wgo_grp[:], wgo_raw[:], 0, P)
-        nc.scalar.copy(out=d, in_=s)
-
+        nc.vector.tensor_copy(
+            out=xj_scales[:, 0, :].bitcast(I32).rearrange("p (i j) -> p i j", i=8),
+            in_=x_scales[:, 0:64].bitcast(I32).unsqueeze(1).to_broadcast([P, 8, 16]),
+        )
+        xd_codes = const.tile([P, P], I32, align_bytes=64)
+        xd_scales = const.tile([P, P], U8, align_bytes=64)
+        nc.vector.tensor_copy(
+            out=xd_codes[:].rearrange("p (i j) -> p i j", i=2),
+            in_=x_codes[:, 192:256].unsqueeze(1).to_broadcast([P, 2, 64]),
+        )
+        nc.vector.tensor_copy(
+            out=xd_scales[:].bitcast(I32).rearrange("p (i j) -> p i j", i=2),
+            in_=x_scales[:, 192:256].bitcast(I32).unsqueeze(1).to_broadcast([P, 2, 16]),
+        )
+        a_out(0, 0, 64)
+        b_out(0)
+        natural_rows()
         first_relation(1)
         ptb_sb = const.tile([P, 256], F32)
 
@@ -206,12 +248,6 @@ def tile_languagemsgencoder_pa_t_kernel(
             pt_ps = psp.tile([P, 256], F32, tag="ps")
             mx(pt_ps[:], wgr_codes[:, 0, :], wgr_scales[:, 0, :], x_codes[:], x_scales[:], True, True)
             nc.scalar.activation(out=ptb_sb[:], in_=pt_ps[:], func=ACT.Identity, bias=bgr_sb[:], scale=1.0)
-            nc.vector.tensor_copy(
-                out=xj_scales[:].rearrange("p b c -> p (b c)").bitcast(I32).rearrange(
-                    "p (b i j) -> p b i j", b=4, i=4),
-                in_=x_scales[:].bitcast(I32).rearrange("p (b j) -> p b j", b=4).unsqueeze(2).to_broadcast(
-                    [P, 4, 4, 16]),
-            )
 
         rel_bf = {}
         rel_codes = {}
@@ -241,33 +277,20 @@ def tile_languagemsgencoder_pa_t_kernel(
                     op=ADD,
                 )
 
-        nat_sb = const.tile([P, 512], F32)
-
-        def natural_rows():
-            na_ps = psp.tile([P, 512], F32, name="na_ps", tag="ps")
-            nb_ps = psp.tile([P, 512], F32, name="nb_ps", tag="ps")
-            for dst, h in ((na_ps, 0), (nb_ps, 1)):
-                mx(dst[:], xj_codes[:, 3, 0:P], xj_scales[:, 3, 0:P], wrel_codes[:, h, :], wrel_scales[:, h, :], True, True)
-            nc.scalar.copy(out=nat_sb[0:64, :], in_=na_ps[0:64, :])
-            nc.scalar.copy(out=nat_sb[64:P, :], in_=nb_ps[64:P, :])
-            nc.scalar.copy(out=nat_sb[0:1, :].rearrange("p (t m) -> p t m", t=4),
-                           in_=brel_row[:].rearrange("p (m t) -> p t m", t=4))
-
         piece_ps = {}
 
         def piece_products(piece):
-            k, q = piece // 4, piece % 4
             rp = psp.tile([P, 4, P], F32, name="rp", tag="ps")
             piece_ps[piece] = rp
             for t in range(4):
-                nc.tensor.matmul(rp[:, t, :], nat_sb[:, t * P:(t + 1) * P], sel[:, k, q * P:(q + 1) * P],
-                                 start=True, stop=True)
+                nc.tensor.matmul(rp[:, t, :], nat_sb[:, t * P:(t + 1) * P],
+                                 sel[:, 2 * piece:2 * piece + 2, :].rearrange("p i j -> p (i j)"), start=True, stop=True)
 
         def piece_out(piece):
             k, q = piece // 4, piece % 4
-            u = (P_TOKENS[k], 8)
+            u = P_UNITS[k]
             if q == 0:
-                rel_bf[u] = relp.tile([P, 2048], BF16, name="rel_p", tag="relP%d" % (k % 2), align_bytes=64)
+                rel_bf[u] = relp.tile([P, u[1] * 256], BF16, name="rel_p", tag="relP%d" % (k % 2), align_bytes=64)
             nc.scalar.copy(out=rel_bf[u][:, q * 512:(q + 1) * 512].rearrange("p (n t) -> p n t", t=4),
                            in_=piece_ps[piece][:].rearrange("p t n -> p n t"))
 
@@ -281,10 +304,11 @@ def tile_languagemsgencoder_pa_t_kernel(
             tok0, n = u
             b = tok0 // 64
             acc = psp.tile([P, n * 64], F32, name="acc", tag="ps")
-            for hf in range(n // 4):
-                cols = slice(hf * 256, (hf + 1) * 256)
-                mx(acc[:, cols], wgr_codes[:, 1, :], wgr_scales[:, 1, :], xj_codes[:, b, :], xj_scales[:, b, :],
-                   True, False)
+            width = n * 64
+            for first in range(0, n * 64, width):
+                cols = slice(first, first + width)
+                mx(acc[:, cols], wgr_codes[:, 1, :], wgr_scales[:, 1, :], xj_codes[:, b, 0:width],
+                   xj_scales[:, b, 0:width], True, False)
                 mx(acc[:, cols], wgr_codes[:, 2, :], wgr_scales[:, 2, :], rel_codes[u][:, cols],
                    rel_scales[u][:, cols], False, True)
             th_sb[u] = thp.tile([P, n * 64], F32, name="th", tag="th")
@@ -340,7 +364,7 @@ def tile_languagemsgencoder_pa_t_kernel(
         cycles = schedule()
         last = len(cycles) - 1
         for c, (v_units, g_units) in enumerate(cycles):
-            p_units = [(P_TOKENS[c // 3 - 1], 8)] if c in (4, 7, 10) else []
+            p_units = tensor_units(c)
             units = p_units + v_units + g_units
             slot_g, slot_v2 = ("relZ", "relY") if c % 2 == 0 else ("relY", "relZ")
             for u in g_units:
@@ -349,28 +373,33 @@ def tile_languagemsgencoder_pa_t_kernel(
                 build(u, False, slot)
             if c == 0:
                 second_stage_operands()
-                natural_rows()
             if c == 1:
-                first_relation_out(1)
-            for piece in pieces_of(c):
+                d, s = permuted_views(wgo_grp[:], wgo_raw[:], 0, P)
+                nc.scalar.copy(out=d, in_=s)
+                a_out(1, 0, P)
+                b_out(1)
+            for piece in range(pieces_built(c - 1), pieces_built(c)):
                 piece_products(piece)
                 piece_out(piece)
-            for u in previous:
+            for k, u in enumerate(previous):
                 turn(u)
-                if c < last:
+                if c < last or k < 2:
                     store(u, False)
             for u in units:
                 quant(u)
                 if c == 1 and u == units[0]:
                     quantise(wgo_codes[:], wgo_scales[:], wgo_grp[:].rearrange("p c t -> p (c t)"))
                     node_update_tanh()
+            if c == 0:
+                a_out(0, 64, P)
             for u in units:
                 product(u)
             if c == last:
-                for u in previous:
+                for u in previous[2:]:
                     store(u, True)
-                turn(units[0])
-                store(units[0], True)
+                for u in units:
+                    turn(u)
+                    store(u, True)
             if c == 2:
                 node_update_out()
             previous = units

from contextlib import ExitStack

import concourse.mybir as mybir
from concourse.masks import make_identity

F32 = mybir.dt.float32
BF16 = mybir.dt.bfloat16
I32 = mybir.dt.int32
U8 = mybir.dt.uint8
FP8X4 = mybir.dt.float8_e4m3fn_x4
ADD = mybir.AluOpType.add
ACT = mybir.ActivationFunctionType

P = 128
FLOPS = 2 * 256 * 512 * (3 * 512 + 2 * 128) + 2 * 16384 * 512 * 128


P_UNITS = ((228, 8), (236, 8), (244, 8), (252, 4))
PIECES = 14


def pieces_built(cycle):
    return min(3 * (cycle + 1) // 2, PIECES) if cycle > 0 else 0


def tensor_units(cycle):
    units = []
    end = 0
    for u in P_UNITS:
        end += u[1] // 2
        if pieces_built(cycle - 2) < end <= pieces_built(cycle - 1):
            units.append(u)
    return units


def schedule():
    cycles = [([(0, 4)], []), ([(4, 4), (16, 8)], [(8, 8)])]
    for c in range(1, 9):
        cycles.append(([(24 * c, 8), (24 * c + 8, 8)], [(24 * c + 16, 8)]))
    cycles.append(([(216, 8)], [(224, 4)]))
    return cycles


def tile_languagemsgencoder_pa_t_kernel(
    tc, text_embedding, W_rel, b_rel, W_go, b_go, W_gr, b_gr, out_0, out_1
):
    nc = tc.nc
    out0_flat = out_0.rearrange("b n d -> (b n) d")
    out1_flat = out_1.rearrange("b i j f -> (b i j) f")

    def mx(out, l_codes, l_scales, r_codes, r_scales, start, stop):
        nc.tensor.matmul_mx(
            out=out,
            lhsT=l_codes.bitcast(FP8X4),
            lhsT_scale=l_scales,
            rhs=r_codes.bitcast(FP8X4),
            rhs_scale=r_scales,
            start=start,
            stop=stop,
        )

    def quantise(codes, scales, grouped):
        nc.vector.quantize_mx(out=codes.bitcast(FP8X4), scales=scales, in_=grouped)

    def regroup_views(dst, src):
        return (
            dst.rearrange("p (c i) t -> p c t i", i=4),
            src.rearrange("p t (c i) -> p c t i", i=4),
        )

    def permuted_views(dst, src, lo, hi):
        return (
            dst.rearrange("p (t m) j -> p t m j", t=4)[:, :, lo:hi, :],
            src.rearrange("p j (m t) -> p t m j", t=4)[:, :, lo:hi, :],
        )

    with ExitStack() as ctx:
        const = ctx.enter_context(tc.tile_pool(name="const", bufs=1))
        relp = ctx.enter_context(tc.tile_pool(name="relp", bufs=1))
        codp = ctx.enter_context(tc.tile_pool(name="codp", bufs=8))
        outp = ctx.enter_context(tc.tile_pool(name="outp", bufs=12))
        thp = ctx.enter_context(tc.tile_pool(name="thp", bufs=8))
        atp = ctx.enter_context(tc.psum_pool(name="atp", bufs=1))
        psp = ctx.enter_context(tc.psum_pool(name="psp", bufs=6))
        ctx.enter_context(tc.manual_schedule())

        x_sb = const.tile([P, 2, 512], BF16)
        wrel_raw = const.tile([P, 8, 512], BF16)
        wgr_raw = const.tile([P, 12, 128], BF16)
        wgo_raw = const.tile([P, 4, 512], BF16)
        brel_sb = const.tile([P, 4], BF16)
        brel_row = const.tile([1, 512], BF16)
        bgo_sb = const.tile([P, 4], BF16)
        bgr_sb = const.tile([P, 1], BF16)
        x_scales = const.tile([P, 256], U8, align_bytes=64)

        nc.vector.memset(x_scales[:].bitcast(I32), 0)

        nc.sync.dma_start(out=wrel_raw[:, 0:4, :], in_=W_rel[0:512, :].rearrange("(p t) c -> p t c", t=4))
        nc.sync.dma_start(
            out=x_sb[:],
            in_=text_embedding.rearrange("b n d -> (b n) d").rearrange("(a p) d -> p a d", p=P),
        )
        nc.sync.dma_start(out=wrel_raw[:, 4:8, :], in_=W_rel[512:1024, :].rearrange("(p t) c -> p t c", t=4))
        nc.sync.dma_start(out=brel_sb[:], in_=b_rel.rearrange("(p t) -> p t", t=4))
        for h in range(3):
            nc.sync.dma_start(
                out=wgr_raw[:, 4 * h:4 * h + 4, :],
                in_=W_gr[512 * h:512 * (h + 1), :].rearrange("(p t) c -> p t c", t=4),
            )
        nc.sync.dma_start(out=wgo_raw[:], in_=W_go.rearrange("(p t) c -> p t c", t=4))
        nc.sync.dma_start(out=bgr_sb[:], in_=b_gr.rearrange("(p o) -> p o", o=1))
        nc.sync.dma_start(out=brel_row[:], in_=b_rel.rearrange("(o c) -> o c", o=1))
        nc.sync.dma_start(out=bgo_sb[:], in_=b_go.rearrange("(p t) -> p t", t=4))

        ident_f = const.tile([P, P], F32)
        make_identity(nc, ident_f[:])
        sel = const.tile([P, 28, 64], F32)
        i0 = P_UNITS[0][0] % 64
        nc.vector.tensor_copy(out=sel[0:64], in_=ident_f[0:64, i0:i0 + 28].unsqueeze(2).to_broadcast([64, 28, 64]))
        nc.vector.tensor_copy(out=sel[64:P], in_=ident_f[64:P, 64:P].unsqueeze(1).to_broadcast([64, 28, 64]))
        nc.vector.memset(sel[0:1], 1.0)

        xt_ps = psp.tile([P, 2, 256], F32, tag="ps")
        for a in range(2):
            words = x_sb[:, a, :].bitcast(F32)
            for u in range(2):
                nc.tensor.transpose(xt_ps[:, u, a * P:(a + 1) * P], words[:, u:256:2], ident_f[:])
        x_grp = const.tile([P, 256, 4], BF16, align_bytes=64)
        x_codes = const.tile([P, 256], I32, align_bytes=64)

        wrel_grp = const.tile([P, 2, 512, 4], BF16, align_bytes=64)
        wrel_codes = const.tile([P, 2, 512], I32, align_bytes=64)
        wrel_scales = const.tile([P, 2, 512], U8, align_bytes=64)
        SPLITS = (48, 40)

        def regroup_wrel(h):
            d, s = permuted_views(wrel_grp[:, h], wrel_raw[:, 4 * h:4 * h + 4, :], 0, SPLITS[h])
            nc.scalar.copy(out=d, in_=s)
            d, s = permuted_views(wrel_grp[:, h], wrel_raw[:, 4 * h:4 * h + 4, :], SPLITS[h], P)
            nc.vector.tensor_copy(out=d, in_=s)

        def quantise_wrel(h):
            quantise(wrel_codes[:, h, :], wrel_scales[:, h, :], wrel_grp[:, h].rearrange("p c t -> p (c t)"))

        regroup_wrel(0)
        nc.scalar.copy(
            out=x_grp[:].rearrange("p n t -> p (n t)").bitcast(F32).rearrange("p (n u) -> p n u", u=2),
            in_=xt_ps[:].rearrange("p u n -> p n u"),
        )
        quantise_wrel(0)
        regroup_wrel(1)
        quantise(x_codes[:], x_scales[:], x_grp[:].rearrange("p n t -> p (n t)"))
        quantise_wrel(1)

        wgr_grp = const.tile([P, 3, 128, 4], BF16, align_bytes=64)
        wgr_codes = const.tile([P, 3, 128], I32, align_bytes=64)
        wgr_scales = const.tile([P, 3, 128], U8, align_bytes=64)

        bt_ps = []
        at_sb = const.tile([P, 256, 4], F32)
        bt_sb = const.tile([P, 256, 4], F32)

        head_ps = {}

        def first_relation(a):
            xc, xs = x_codes[:, a * P:(a + 1) * P], x_scales[:, a * P:(a + 1) * P]
            bt_a = atp.tile([P, 4, P], F32, name="bt%d" % a)
            bt_ps.append(bt_a)
            at_tmp = psp.tile([P, 4, P], F32, name="at_tmp", tag="ps")
            targets = [(at_tmp, 0), (bt_a, 1)]
            if a == 0:
                bt_tmp = psp.tile([P, 4, P], F32, name="bt_tmp", tag="ps")
                targets.append((bt_tmp, 1))
            head_ps[a] = (at_tmp, bt_tmp if a == 0 else bt_a)
            for dst, h in targets:
                for t in range(4):
                    mx(dst[:, t, :], wrel_codes[:, h, t * P:(t + 1) * P], wrel_scales[:, h, t * P:(t + 1) * P],
                       xc, xs, True, True)

        def a_out(a, lo, hi):
            nc.vector.tensor_tensor(
                out=at_sb[:, a * P + lo:a * P + hi, :],
                in0=head_ps[a][0][:, :, lo:hi].rearrange("p t n -> p n t"),
                in1=brel_sb[:].unsqueeze(1).to_broadcast([P, hi - lo, 4]),
                op=ADD,
            )

        def b_out(a):
            nc.scalar.copy(out=bt_sb[:, a * P:(a + 1) * P, :], in_=head_ps[a][1][:].rearrange("p t n -> p n t"))

        nat_sb = const.tile([P, 512], F32)

        def natural_rows():
            na_ps = psp.tile([P, 512], F32, name="na_ps", tag="ps")
            nb_ps = psp.tile([P, 512], F32, name="nb_ps", tag="ps")
            for dst, h in ((na_ps, 0), (nb_ps, 1)):
                mx(dst[:], xd_codes[:], xd_scales[:], wrel_codes[:, h, :], wrel_scales[:, h, :], True, True)
            nc.scalar.copy(out=nat_sb[0:64, :], in_=na_ps[0:64, :])
            nc.scalar.copy(out=nat_sb[64:P, :], in_=nb_ps[64:P, :])
            nc.scalar.copy(out=nat_sb[0:1, :].rearrange("p (t m) -> p t m", t=4),
                           in_=brel_row[:].rearrange("p (m t) -> p t m", t=4))

        wgo_grp = const.tile([P, 512, 4], BF16, align_bytes=64)
        for h in range(3):
            d, s = regroup_views(wgr_grp[:, h], wgr_raw[:, 4 * h:4 * h + 4, :])
            nc.scalar.copy(out=d, in_=s)

        first_relation(0)
        xj_codes = const.tile([P, 4, 512], I32, align_bytes=64)
        xj_scales = const.tile([P, 4, 512], U8, align_bytes=64)
        for b in range(1, 4):
            nc.sync.dma_start(
                out=xj_codes[:, b, :].rearrange("p (i j) -> p i j", i=8),
                in_=x_codes[:, 64 * b:64 * (b + 1)].unsqueeze(1).to_broadcast([P, 8, 64]),
            )
            nc.sync.dma_start(
                out=xj_scales[:, b, :].bitcast(I32).rearrange("p (i j) -> p i j", i=8),
                in_=x_scales[:, 64 * b:64 * (b + 1)].bitcast(I32).unsqueeze(1).to_broadcast([P, 8, 16]),
            )
        nc.vector.tensor_copy(
            out=xj_codes[:, 0, :].rearrange("p (i j) -> p i j", i=8),
            in_=x_codes[:, 0:64].unsqueeze(1).to_broadcast([P, 8, 64]),
        )
        nc.vector.tensor_copy(
            out=xj_scales[:, 0, :].bitcast(I32).rearrange("p (i j) -> p i j", i=8),
            in_=x_scales[:, 0:64].bitcast(I32).unsqueeze(1).to_broadcast([P, 8, 16]),
        )
        xd_codes = const.tile([P, P], I32, align_bytes=64)
        xd_scales = const.tile([P, P], U8, align_bytes=64)
        nc.vector.tensor_copy(
            out=xd_codes[:].rearrange("p (i j) -> p i j", i=2),
            in_=x_codes[:, 192:256].unsqueeze(1).to_broadcast([P, 2, 64]),
        )
        nc.vector.tensor_copy(
            out=xd_scales[:].bitcast(I32).rearrange("p (i j) -> p i j", i=2),
            in_=x_scales[:, 192:256].bitcast(I32).unsqueeze(1).to_broadcast([P, 2, 16]),
        )
        a_out(0, 0, 64)
        b_out(0)
        natural_rows()
        first_relation(1)
        ptb_sb = const.tile([P, 256], F32)

        def second_stage_operands():
            for h in range(3):
                quantise(wgr_codes[:, h, :], wgr_scales[:, h, :], wgr_grp[:, h].rearrange("p c t -> p (c t)"))
            pt_ps = psp.tile([P, 256], F32, tag="ps")
            mx(pt_ps[:], wgr_codes[:, 0, :], wgr_scales[:, 0, :], x_codes[:], x_scales[:], True, True)
            nc.scalar.activation(out=ptb_sb[:], in_=pt_ps[:], func=ACT.Identity, bias=bgr_sb[:], scale=1.0)

        rel_bf = {}
        rel_codes = {}
        rel_scales = {}
        th_sb = {}

        def build(u, on_gpsimd, slot):
            tok0, n = u
            b = tok0 // 64
            c0 = (b % 2) * 64
            in0 = at_sb[:, tok0:tok0 + n, :].unsqueeze(2).to_broadcast([P, n, 64, 4])
            if on_gpsimd:
                rel_bf[u] = relp.tile([P, n * 256], BF16, name="rel_g", tag=slot, align_bytes=64)
                nc.gpsimd.tensor_tensor(
                    out=rel_bf[u][:].rearrange("p (i j t) -> p i j t", i=n, j=64),
                    in0=in0,
                    in1=bt_sb[:, b * 64:(b + 1) * 64, :].unsqueeze(1).to_broadcast([P, n, 64, 4]),
                    op=ADD,
                )
            else:
                rel_bf[u] = relp.tile([P, n * 256], BF16, name="rel_v", tag=slot, align_bytes=64)
                nc.vector.tensor_tensor(
                    out=rel_bf[u][:].rearrange("p (i j t) -> p i j t", i=n, j=64),
                    in0=in0,
                    in1=bt_ps[b // 2][:, :, c0:c0 + 64].rearrange("p t j -> p j t").unsqueeze(1).to_broadcast(
                        [P, n, 64, 4]),
                    op=ADD,
                )

        piece_ps = {}

        def piece_products(piece):
            rp = psp.tile([P, 4, P], F32, name="rp", tag="ps")
            piece_ps[piece] = rp
            for t in range(4):
                nc.tensor.matmul(rp[:, t, :], nat_sb[:, t * P:(t + 1) * P],
                                 sel[:, 2 * piece:2 * piece + 2, :].rearrange("p i j -> p (i j)"), start=True, stop=True)

        def piece_out(piece):
            k, q = piece // 4, piece % 4
            u = P_UNITS[k]
            if q == 0:
                rel_bf[u] = relp.tile([P, u[1] * 256], BF16, name="rel_p", tag="relP%d" % (k % 2), align_bytes=64)
            nc.scalar.copy(out=rel_bf[u][:, q * 512:(q + 1) * 512].rearrange("p (n t) -> p n t", t=4),
                           in_=piece_ps[piece][:].rearrange("p t n -> p n t"))

        def quant(u):
            n = u[1]
            rel_codes[u] = codp.tile([P, n * 64], I32, name="rel_codes", tag="rel_codes", align_bytes=64)
            rel_scales[u] = codp.tile([P, n * 64], U8, name="rel_scales", tag="rel_scales", align_bytes=64)
            quantise(rel_codes[u][:], rel_scales[u][:], rel_bf[u][:])

        def product(u):
            tok0, n = u
            b = tok0 // 64
            acc = psp.tile([P, n * 64], F32, name="acc", tag="ps")
            width = n * 64
            for first in range(0, n * 64, width):
                cols = slice(first, first + width)
                mx(acc[:, cols], wgr_codes[:, 1, :], wgr_scales[:, 1, :], xj_codes[:, b, 0:width],
                   xj_scales[:, b, 0:width], True, False)
                mx(acc[:, cols], wgr_codes[:, 2, :], wgr_scales[:, 2, :], rel_codes[u][:, cols],
                   rel_scales[u][:, cols], False, True)
            th_sb[u] = thp.tile([P, n * 64], F32, name="th", tag="th")
            for i in range(n):
                tok = tok0 + i
                nc.scalar.activation(out=th_sb[u][:, i * 64:(i + 1) * 64], in_=acc[:, i * 64:(i + 1) * 64],
                                     func=ACT.Tanh, bias=ptb_sb[:, tok:tok + 1], scale=1.0)

        tr_ps = {}

        def turn(u):
            n = u[1]
            tr_ps[u] = psp.tile([P, n * 64], F32, name="tr", tag="ps")
            for k in range(n // 2):
                nc.tensor.transpose(tr_ps[u][:, k * P:(k + 1) * P], th_sb[u][:, k * P:(k + 1) * P], ident_f[:])

        def store(u, on_vector):
            tok0, n = u
            tr = tr_ps[u]
            o_sb = outp.tile([P, n // 2, P], F32, name="o_sb", tag="o_sb")
            if on_vector:
                nc.vector.tensor_copy(out=o_sb[:].rearrange("p k f -> p (k f)"), in_=tr[:])
            else:
                nc.scalar.copy(out=o_sb[:].rearrange("p k f -> p (k f)"), in_=tr[:])
            nc.sync.dma_start(
                out=out1_flat[tok0 * 64:(tok0 + n) * 64, :].rearrange("(k m) f -> m k f", m=P), in_=o_sb[:]
            )

        wgo_codes = const.tile([P, 512], I32, align_bytes=64)
        wgo_scales = const.tile([P, 512], U8, align_bytes=64)
        nxt_sb = const.tile([P, 4, 256], F32)

        def node_update_tanh():
            for t in range(4):
                nx_ps = psp.tile([P, 256], F32, name="nx_ps", tag="ps")
                mx(nx_ps[:], wgo_codes[:, t * P:(t + 1) * P], wgo_scales[:, t * P:(t + 1) * P],
                   x_codes[:], x_scales[:], True, True)
                nc.scalar.activation(out=nxt_sb[:, t, :], in_=nx_ps[:], func=ACT.Tanh,
                                     bias=bgo_sb[:, t:t + 1], scale=1.0)

        def node_update_out():
            for a in range(2):
                nxr_ps = psp.tile([P, 512], F32, name="nxr_ps", tag="ps")
                for t in range(4):
                    nc.tensor.transpose(nxr_ps[:, t * P:(t + 1) * P], nxt_sb[:, t, a * P:(a + 1) * P], ident_f[:])
                nx_sb = outp.tile([P, 512], F32, name="nx_sb", tag="nx_sb")
                nc.scalar.copy(
                    out=nx_sb[:].rearrange("p (m t) -> p m t", t=4), in_=nxr_ps[:].rearrange("p (t m) -> p m t", t=4)
                )
                nc.sync.dma_start(out=out0_flat[a * P:(a + 1) * P, :], in_=nx_sb[:])

        previous = []
        cycles = schedule()
        last = len(cycles) - 1
        for c, (v_units, g_units) in enumerate(cycles):
            p_units = tensor_units(c)
            units = p_units + v_units + g_units
            slot_g, slot_v2 = ("relZ", "relY") if c % 2 == 0 else ("relY", "relZ")
            for u in g_units:
                build(u, True, slot_g)
            for u, slot in zip(v_units, ("relX", slot_v2) if len(v_units) == 2 else (slot_v2,)):
                build(u, False, slot)
            if c == 0:
                second_stage_operands()
            if c == 1:
                d, s = permuted_views(wgo_grp[:], wgo_raw[:], 0, P)
                nc.scalar.copy(out=d, in_=s)
                a_out(1, 0, P)
                b_out(1)
            for piece in range(pieces_built(c - 1), pieces_built(c)):
                piece_products(piece)
                piece_out(piece)
            for k, u in enumerate(previous):
                turn(u)
                if c < last or k < 2:
                    store(u, False)
            for u in units:
                quant(u)
                if c == 1 and u == units[0]:
                    quantise(wgo_codes[:], wgo_scales[:], wgo_grp[:].rearrange("p c t -> p (c t)"))
                    node_update_tanh()
            if c == 0:
                a_out(0, 64, P)
            for u in units:
                product(u)
            if c == last:
                for u in previous[2:]:
                    store(u, True)
                for u in units:
                    turn(u)
                    store(u, True)
            if c == 2:
                node_update_out()
            previous = units
